import numpy as np
import ml_dtypes


def mxq(x, axis, fmt="e4m3"):
    dtype, down = {"e4m3": (ml_dtypes.float8_e4m3fn, 7), "e5m2": (ml_dtypes.float8_e5m2, 14)}[fmt]
    v = np.moveaxis(np.asarray(x, np.float32).astype(ml_dtypes.bfloat16).astype(np.float64), axis, -1)
    blocks = v.reshape(v.shape[:-1] + (-1, 32))
    amax = np.abs(blocks).max(-1, keepdims=True)
    byte = np.maximum(np.where(amax > 0, np.frexp(amax)[1] - 1 + 127, 0) - down, 1)
    scale = np.exp2(byte - 127.0)
    codes = (blocks / scale).astype(np.float32).astype(dtype).astype(np.float64)
    return np.moveaxis((codes * scale).reshape(v.shape), -1, axis)


WIDE = False


def mx_kscale(k):
    if not WIDE:
        return np.ones(k)
    levels = np.array([10, -10, 5, -5, 0])
    a = np.random.permutation(np.resize(levels, k // 512 * 4)).reshape(k // 512, 4)
    idx = np.arange(k)
    return np.exp2(a[idx // 512, idx % 128 // 32])


BF16 = ml_dtypes.bfloat16


def bf(x):
    return np.asarray(x, np.float32).astype(BF16)


def f64(x):
    return np.asarray(x).astype(np.float64)


B, LQ, LY, D = 2, 4096, 512, 1024
EPS = 1e-8


def setup_inputs():
    r, u = mx_kscale(LQ), mx_kscale(LY)
    g = D ** -0.25
    c = np.random.standard_normal((B, 1, D))
    aq = np.random.standard_normal((B, LQ, 1))
    ay = np.random.standard_normal((B, LY, 1))
    return {"query": bf((np.random.standard_normal((B, LQ, D)) + aq * c) * g * r[:, None]),
            "y": bf((np.random.standard_normal((B, LY, D)) + ay * c) * g * u[:, None])}


def reference(query, y):
    q, k = f64(query), f64(y)
    dots = mxq(q, 2, "e4m3") @ mxq(k, 2, "e4m3").transpose(0, 2, 1)
    nq = np.linalg.norm(q, axis=-1)
    ny = np.linalg.norm(k, axis=-1)
    denom = np.maximum(nq[:, :, None] * ny[:, None, :], EPS)
    att = dots / denom
    sim = att.max(axis=2)[:, None, :]
    e = np.exp(att - att.max(axis=2, keepdims=True))
    att = e / e.sum(axis=2, keepdims=True)
    return att, sim

@@ -1,0 +1,293 @@
+from contextlib import ExitStack
+
+import concourse.mybir as mybir
+from concourse.masks import make_identity
+
+F32 = mybir.dt.float32
+BF16 = mybir.dt.bfloat16
+U32 = mybir.dt.uint32
+U8 = mybir.dt.uint8
+FP8X4 = mybir.dt.float8_e4m3fn_x4
+ALU = mybir.AluOpType
+ACT = mybir.ActivationFunctionType
+
+B, LQ, LY, D = 2, 4096, 512, 1024
+EPS = 1e-8
+TINY = 1e-36
+
+P = 128
+PACK = 4
+K_PASS = P * PACK
+PASSES = D // K_PASS
+HALVES = 2
+BLOCKS = PASSES * HALVES
+GROUP = 4
+TILES = LQ // P
+GROUPS = TILES // GROUP
+WORDS = GROUP * PASSES * P
+
+FLOPS = 2 * B * LQ * LY * D
+
+
+def tile_attcosine_t_kernel(tc, query, y, out_0, out_1):
+    nc = tc.nc
+    assert LY == GROUP * P
+
+    q_view = [query[b].rearrange("(p s) d -> p s d", s=TILES) for b in range(B)]
+    att_view = [out_0[b].rearrange("(p s) j -> p s j", s=TILES) for b in range(B)]
+    sim_view = [out_1[b, 0].rearrange("(p s) -> p s", s=TILES) for b in range(B)]
+    y_view = [y[b].rearrange("(t p) d -> p t d", p=P) for b in range(B)]
+
+    items = []
+    for b in range(B):
+        items.append({"b": b, "g": None})
+        for g in range(GROUPS):
+            items.append({"b": b, "g": g})
+    keys = [{} for b in range(B)]
+
+    def is_keys(i):
+        return 0 <= i < len(items) and items[i]["g"] is None
+
+    def is_queries(i):
+        return 0 <= i < len(items) and items[i]["g"] is not None
+
+    with ExitStack() as ctx:
+        consts = ctx.enter_context(tc.tile_pool(name="consts", bufs=1))
+        key_keep = ctx.enter_context(tc.tile_pool(name="key_keep", bufs=B))
+        spread = ctx.enter_context(tc.tile_pool(name="spread", bufs=GROUP))
+        loads = ctx.enter_context(tc.tile_pool(name="loads", bufs=5))
+        squares = ctx.enter_context(tc.tile_pool(name="squares", bufs=4))
+        packed = ctx.enter_context(tc.tile_pool(name="packed", bufs=2))
+        small = ctx.enter_context(tc.tile_pool(name="small", bufs=6))
+        work = ctx.enter_context(tc.tile_pool(name="work", bufs=2))
+        stores = ctx.enter_context(tc.tile_pool(name="stores", bufs=3))
+        turn_banks = ctx.enter_context(tc.psum_pool(name="turn_banks", bufs=GROUP))
+        dot_banks = ctx.enter_context(tc.psum_pool(name="dot_banks", bufs=GROUP))
+        ctx.enter_context(tc.manual_schedule())
+
+        identity = consts.tile([P, P], F32)
+        make_identity(nc, identity[:])
+        exponents = consts.tile([P, 2 * GROUP], F32)
+        nc.gpsimd.memset(exponents[:, 0:GROUP], -0.5)
+        nc.gpsimd.memset(exponents[:, GROUP : 2 * GROUP], 0.5)
+
+        def load(i):
+            b, g = items[i]["b"], items[i]["g"]
+            rows = loads.tile([P, GROUP, D], BF16)
+            if g is None:
+                nc.sync.dma_start(out=rows[:], in_=y_view[b])
+            else:
+                nc.sync.dma_start(out=rows[:], in_=q_view[b][:, g * GROUP : (g + 1) * GROUP, :])
+            items[i]["rows"] = rows
+
+        def turn(i):
+            banks = []
+            for t in range(GROUP):
+                words = items[i]["rows"][:, t, :].bitcast(F32)
+                bank = turn_banks.tile([P, BLOCKS, P], F32)
+                for c in range(BLOCKS):
+                    nc.tensor.transpose(bank[:, c, :], words[:, c * P : (c + 1) * P], identity[:])
+                banks.append(bank)
+            items[i]["banks"] = banks
+
+        def regroup(i):
+            grouped = packed.tile([P, WORDS * PACK], BF16, align_bytes=64)
+            order = "p (k t r u) -> p t k r u" if is_keys(i) else "p (t k r u) -> p t k r u"
+            grouped_words = grouped[:].bitcast(F32).rearrange(
+                order, t=GROUP, k=PASSES, u=HALVES
+            )
+            for t in range(GROUP):
+                copy = nc.scalar.copy if t == GROUP - 1 else nc.vector.tensor_copy
+                copy(
+                    out=grouped_words[:, t],
+                    in_=items[i]["banks"][t][:].rearrange("p (k u) r -> p k r u", u=HALVES),
+                )
+            items[i]["grouped"] = grouped
+
+        def sums_of_squares(i):
+            sums = small.tile([P, GROUP], F32)
+            for t in range(GROUP):
+                squared = squares.tile([P, D], BF16)
+                nc.scalar.activation(
+                    out=squared[:],
+                    in_=items[i]["rows"][:, t, :],
+                    func=ACT.Square,
+                    accum_out=sums[:, t : t + 1],
+                )
+            return sums
+
+        def key_norms(i):
+            sums = sums_of_squares(i)
+            floored = small.tile([P, GROUP], F32)
+            nc.gpsimd.tensor_scalar_max(out=floored[:], in0=sums[:], scalar1=TINY)
+            inverse = small.tile([P, GROUP], F32)
+            nc.gpsimd.tensor_tensor(
+                out=inverse[:], in0=floored[:], in1=exponents[:, 0:GROUP], op=ALU.pow
+            )
+            items[i]["inverse"] = inverse
+
+        def query_norms(i):
+            sums = sums_of_squares(i)
+            bases = small.tile([P, 2 * GROUP], F32)
+            nc.gpsimd.tensor_scalar_max(out=bases[:, 0:GROUP], in0=sums[:], scalar1=TINY)
+            nc.gpsimd.tensor_scalar(
+                out=bases[:, GROUP : 2 * GROUP],
+                in0=sums[:],
+                scalar1=TINY,
+                scalar2=1.0 / (EPS * EPS),
+                op0=ALU.max,
+                op1=ALU.mult,
+            )
+            roots = small.tile([P, 2 * GROUP], F32)
+            nc.gpsimd.tensor_tensor(out=roots[:], in0=bases[:], in1=exponents[:], op=ALU.pow)
+            items[i]["inverse_nq"] = roots[:, 0:GROUP]
+            items[i]["ceiling"] = roots[:, GROUP : 2 * GROUP]
+
+        def quantise(i):
+            pool = key_keep if is_keys(i) else packed
+            codes = pool.tile([P, WORDS], U32, align_bytes=64)
+            scales = pool.tile([P, WORDS], U8, align_bytes=64)
+            nc.vector.quantize_mx(
+                out=codes[:].bitcast(FP8X4), scales=scales[:], in_=items[i]["grouped"][:]
+            )
+            items[i]["codes"] = codes
+            items[i]["scales"] = scales
+
+        def spread_key_norms(i):
+            bank = dot_banks.tile([P, GROUP, P], F32, tag="dots")
+            for t in range(GROUP):
+                repeated = spread.tile([P, P], F32)
+                nc.vector.tensor_copy(
+                    out=repeated[:], in_=items[i]["inverse"][:, t : t + 1].to_broadcast([P, P])
+                )
+                nc.tensor.transpose(bank[:, t, :], repeated[:], identity[:])
+            items[i]["spread"] = bank
+
+        def keep_keys(i):
+            inverse_ny = key_keep.tile([P, LY], F32)
+            nc.vector.tensor_copy(
+                out=inverse_ny[:], in_=items[i]["spread"][:].rearrange("p t j -> p (t j)")
+            )
+            negative_shift = key_keep.tile([P, TILES], F32)
+            side = keys[items[i]["b"]]
+            side["codes"] = items[i]["codes"]
+            side["scales"] = items[i]["scales"]
+            side["inverse_ny"] = inverse_ny
+            side["negative_shift"] = negative_shift
+
+        def multiply(i):
+            side = keys[items[i]["b"]]
+            banks = []
+            for t in range(GROUP):
+                dots = dot_banks.tile([P, LY], F32, tag="dots")
+                for k in range(PASSES):
+                    q_cols = slice((t * PASSES + k) * P, (t * PASSES + k + 1) * P)
+                    y_cols = slice(k * LY, (k + 1) * LY)
+                    nc.tensor.matmul_mx(
+                        out=dots[:],
+                        lhsT=items[i]["codes"][:, q_cols].bitcast(FP8X4),
+                        lhsT_scale=items[i]["scales"][:, q_cols],
+                        rhs=side["codes"][:, y_cols].bitcast(FP8X4),
+                        rhs_scale=side["scales"][:, y_cols],
+                        start=(k == 0),
+                        stop=(k == PASSES - 1),
+                    )
+                banks.append(dots)
+            items[i]["dots"] = banks
+
+        def scale(i):
+            side, g = keys[items[i]["b"]], items[i]["g"]
+            scaled = work.tile([P, GROUP, LY], F32)
+            for t in range(GROUP):
+                nc.vector.scalar_tensor_tensor(
+                    out=scaled[:, t, :],
+                    in0=side["inverse_ny"][:],
+                    scalar=items[i]["ceiling"][:, t : t + 1],
+                    in1=items[i]["dots"][t][:],
+                    op0=ALU.min,
+                    op1=ALU.mult,
+                )
+            negative_top = small.tile([P, GROUP], F32)
+            nc.vector.tensor_reduce(
+                out=negative_top[:],
+                in_=scaled[:],
+                axis=mybir.AxisListType.X,
+                op=ALU.max,
+                negate=True,
+            )
+            nc.vector.tensor_mul(
+                out=side["negative_shift"][:, g * GROUP : (g + 1) * GROUP],
+                in0=negative_top[:],
+                in1=items[i]["inverse_nq"],
+            )
+            items[i]["scaled"] = scaled
+
+        def exponentials(i):
+            side, g = keys[items[i]["b"]], items[i]["g"]
+            raised = work.tile([P, GROUP, LY], F32)
+            row_sums = small.tile([P, GROUP], F32)
+            for t in range(GROUP):
+                column = g * GROUP + t
+                nc.scalar.activation(
+                    out=raised[:, t, :],
+                    in_=items[i]["scaled"][:, t, :],
+                    func=ACT.Exp,
+                    bias=side["negative_shift"][:, column : column + 1],
+                    scale=items[i]["inverse_nq"][:, t : t + 1],
+                    accum_out=row_sums[:, t : t + 1],
+                )
+            items[i]["raised"] = raised
+            items[i]["row_sums"] = row_sums
+
+        def invert_row_sums(i):
+            inverse_sums = small.tile([P, GROUP], F32)
+            nc.vector.reciprocal(out=inverse_sums[:], in_=items[i]["row_sums"][:])
+            items[i]["inverse_sums"] = inverse_sums
+
+        def finish(i):
+            b, g = items[i]["b"], items[i]["g"]
+            att = stores.tile([P, GROUP, LY], F32)
+            for t in range(GROUP):
+                nc.gpsimd.tensor_scalar(
+                    out=att[:, t, :],
+                    in0=items[i]["raised"][:, t, :],
+                    scalar1=items[i]["inverse_sums"][:, t : t + 1],
+                    scalar2=0.0,
+                    op0=ALU.mult,
+                    op1=ALU.add,
+                )
+            nc.sync.dma_start(out=att_view[b][:, g * GROUP : (g + 1) * GROUP, :], in_=att[:])
+            if g == GROUPS - 1:
+                sim = stores.tile([P, TILES], F32)
+                nc.vector.tensor_scalar_mul(
+                    out=sim[:], in0=keys[b]["negative_shift"][:], scalar1=-1.0
+                )
+                nc.sync.dma_start(out=sim_view[b], in_=sim[:])
+
+        for s in range(-3, len(items) + 5):
+            if is_keys(s + 3) or is_queries(s + 3):
+                load(s + 3)
+            if is_keys(s - 1) or is_queries(s - 1):
+                regroup(s - 1)
+            if is_keys(s) or is_queries(s):
+                turn(s)
+            if is_queries(s - 5):
+                invert_row_sums(s - 5)
+            if is_keys(s - 2) or is_queries(s - 2):
+                quantise(s - 2)
+            if is_keys(s - 3):
+                keep_keys(s - 3)
+            if is_queries(s - 3):
+                scale(s - 3)
+            if is_keys(s - 2):
+                spread_key_norms(s - 2)
+            if is_queries(s - 2):
+                multiply(s - 2)
+            if is_queries(s - 4):
+                exponentials(s - 4)
+            if is_queries(s - 5):
+                finish(s - 5)
+            if is_keys(s - 1):
+                key_norms(s - 1)
+            if is_queries(s - 1):
+                query_norms(s - 1)

@@ -23,6 +23,7 @@ HALVES = 2
 BLOCKS = PASSES * HALVES
 GROUP = 4
 TILES = LQ // P
+EARLY, SHARE, LATE = 12, 7, 66
 GROUPS = TILES // GROUP
 WORDS = GROUP * PASSES * P
 
@@ -43,105 +44,141 @@ def tile_attcosine_t_kernel(tc, query, y, out_0, out_1):
         items.append({"b": b, "g": None})
         for g in range(GROUPS):
             items.append({"b": b, "g": g})
+    last = len(items) - 1
     keys = [{} for b in range(B)]
 
     def is_keys(i):
-        return 0 <= i < len(items) and items[i]["g"] is None
+        return items[i]["g"] is None
 
-    def is_queries(i):
-        return 0 <= i < len(items) and items[i]["g"] is not None
+    def on_tensor(i, t):
+        if is_keys(i):
+            return False
+        return t == 0 or (t == 2 and items[i]["g"] % 2 == 0)
 
     with ExitStack() as ctx:
         consts = ctx.enter_context(tc.tile_pool(name="consts", bufs=1))
         key_keep = ctx.enter_context(tc.tile_pool(name="key_keep", bufs=B))
-        spread = ctx.enter_context(tc.tile_pool(name="spread", bufs=GROUP))
         loads = ctx.enter_context(tc.tile_pool(name="loads", bufs=5))
         squares = ctx.enter_context(tc.tile_pool(name="squares", bufs=4))
-        packed = ctx.enter_context(tc.tile_pool(name="packed", bufs=2))
-        small = ctx.enter_context(tc.tile_pool(name="small", bufs=6))
-        work = ctx.enter_context(tc.tile_pool(name="work", bufs=2))
-        stores = ctx.enter_context(tc.tile_pool(name="stores", bufs=3))
-        turn_banks = ctx.enter_context(tc.psum_pool(name="turn_banks", bufs=GROUP))
+        packed = ctx.enter_context(tc.tile_pool(name="packed", bufs=3))
+        small = ctx.enter_context(tc.tile_pool(name="small", bufs=8))
+        work = ctx.enter_context(tc.tile_pool(name="work", bufs=4))
+        stores = ctx.enter_context(tc.tile_pool(name="stores", bufs=5))
+        turn_banks = ctx.enter_context(tc.psum_pool(name="turn_banks", bufs=3))
+        gram_banks = ctx.enter_context(tc.psum_pool(name="gram_banks", bufs=1))
         dot_banks = ctx.enter_context(tc.psum_pool(name="dot_banks", bufs=GROUP))
         ctx.enter_context(tc.manual_schedule())
 
         identity = consts.tile([P, P], F32)
         make_identity(nc, identity[:])
-        exponents = consts.tile([P, 2 * GROUP], F32)
-        nc.gpsimd.memset(exponents[:, 0:GROUP], -0.5)
-        nc.gpsimd.memset(exponents[:, GROUP : 2 * GROUP], 0.5)
+        exponents = consts.tile([P, GROUP], F32)
+        nc.gpsimd.memset(exponents[:], -0.5)
 
         def load(i):
             b, g = items[i]["b"], items[i]["g"]
             rows = loads.tile([P, GROUP, D], BF16)
-            if g is None:
+            if i == 0:
+                for t in range(GROUP):
+                    nc.sync.dma_start(out=rows[:, t, :], in_=y_view[b][:, t, :])
+            elif g is None:
                 nc.sync.dma_start(out=rows[:], in_=y_view[b])
             else:
                 nc.sync.dma_start(out=rows[:], in_=q_view[b][:, g * GROUP : (g + 1) * GROUP, :])
-            items[i]["rows"] = rows
-
-        def turn(i):
-            banks = []
-            for t in range(GROUP):
-                words = items[i]["rows"][:, t, :].bitcast(F32)
-                bank = turn_banks.tile([P, BLOCKS, P], F32)
-                for c in range(BLOCKS):
-                    nc.tensor.transpose(bank[:, c, :], words[:, c * P : (c + 1) * P], identity[:])
-                banks.append(bank)
-            items[i]["banks"] = banks
-
-        def regroup(i):
-            grouped = packed.tile([P, WORDS * PACK], BF16, align_bytes=64)
-            order = "p (k t r u) -> p t k r u" if is_keys(i) else "p (t k r u) -> p t k r u"
-            grouped_words = grouped[:].bitcast(F32).rearrange(
-                order, t=GROUP, k=PASSES, u=HALVES
-            )
-            for t in range(GROUP):
-                copy = nc.scalar.copy if t == GROUP - 1 else nc.vector.tensor_copy
-                copy(
-                    out=grouped_words[:, t],
-                    in_=items[i]["banks"][t][:].rearrange("p (k u) r -> p k r u", u=HALVES),
-                )
-            items[i]["grouped"] = grouped
-
-        def sums_of_squares(i):
             sums = small.tile([P, GROUP], F32)
-            for t in range(GROUP):
-                squared = squares.tile([P, D], BF16)
-                nc.scalar.activation(
-                    out=squared[:],
-                    in_=items[i]["rows"][:, t, :],
-                    func=ACT.Square,
-                    accum_out=sums[:, t : t + 1],
-                )
-            return sums
+            items[i]["rows"] = rows
+            items[i]["sums"] = sums
+            items[i]["banks"] = {}
+            items[i]["dots"] = {}
 
-        def key_norms(i):
-            sums = sums_of_squares(i)
+        def turn(i, t):
+            words = items[i]["rows"][:, t, :].bitcast(F32)
+            bank = turn_banks.tile([P, BLOCKS, P], F32)
+            for c in range(BLOCKS):
+                nc.tensor.transpose(bank[:, c, :], words[:, c * P : (c + 1) * P], identity[:])
+            items[i]["banks"][t] = bank
+
+        def grouped_order(i):
+            return "p (k t r u) -> p t k r u" if is_keys(i) else "p (t k r u) -> p t k r u"
+
+        def regroup(i, t):
+            if t == 0:
+                items[i]["grouped"] = packed.tile(
+                    [P, WORDS * PACK], BF16, align_bytes=64, name="grouped"
+                )
+            grouped_words = items[i]["grouped"][:].bitcast(F32).rearrange(
+                grouped_order(i), t=GROUP, k=PASSES, u=HALVES
+            )
+            n = GROUP * i + t
+            on_scalar = n >= EARLY and (n * SHARE) % 8 < SHARE or n >= LATE
+            copy = nc.scalar.copy if on_scalar else nc.vector.tensor_copy
+            copy(
+                out=grouped_words[:, t],
+                in_=items[i]["banks"][t][:].rearrange("p (k u) r -> p k r u", u=HALVES),
+            )
+
+        def square(i, t):
+            squared = squares.tile([P, D], BF16)
+            nc.scalar.activation(
+                out=squared[:],
+                in_=items[i]["rows"][:, t, :],
+                func=ACT.Square,
+                accum_out=items[i]["sums"][:, t : t + 1],
+            )
+
+        def gram(i, t):
+            values = items[i]["grouped"][:].rearrange(
+                grouped_order(i).replace("u", "w"), t=GROUP, k=PASSES, w=PACK
+            )
+            if t == 0:
+                items[i]["gram"] = gram_banks.tile([P, GROUP, P], F32, name="gram")
+            for k in range(PASSES):
+                for w in range(PACK):
+                    x = values[:, t, k, :, w]
+                    nc.tensor.matmul(
+                        items[i]["gram"][:, t, :],
+                        lhsT=x,
+                        rhs=x,
+                        start=(k == 0 and w == 0),
+                        stop=(k == PASSES - 1 and w == PACK - 1),
+                    )
+
+        def diagonal(i):
+            for t in range(GROUP):
+                if on_tensor(i, t):
+                    masked = squares.tile([P, P], F32)
+                    nc.vector.scalar_tensor_tensor(
+                        out=masked[:],
+                        in0=items[i]["gram"][:, t, :],
+                        scalar=1.0,
+                        in1=identity[:],
+                        op0=ALU.mult,
+                        op1=ALU.mult,
+                        accum_out=items[i]["sums"][:, t : t + 1],
+                    )
+
+        def norms(i):
             floored = small.tile([P, GROUP], F32)
-            nc.gpsimd.tensor_scalar_max(out=floored[:], in0=sums[:], scalar1=TINY)
+            nc.gpsimd.tensor_scalar_max(out=floored[:], in0=items[i]["sums"][:], scalar1=TINY)
             inverse = small.tile([P, GROUP], F32)
             nc.gpsimd.tensor_tensor(
-                out=inverse[:], in0=floored[:], in1=exponents[:, 0:GROUP], op=ALU.pow
+                out=inverse[:], in0=floored[:], in1=exponents[:], op=ALU.pow
             )
             items[i]["inverse"] = inverse
-
-        def query_norms(i):
-            sums = sums_of_squares(i)
-            bases = small.tile([P, 2 * GROUP], F32)
-            nc.gpsimd.tensor_scalar_max(out=bases[:, 0:GROUP], in0=sums[:], scalar1=TINY)
-            nc.gpsimd.tensor_scalar(
-                out=bases[:, GROUP : 2 * GROUP],
-                in0=sums[:],
-                scalar1=TINY,
-                scalar2=1.0 / (EPS * EPS),
-                op0=ALU.max,
-                op1=ALU.mult,
-            )
-            roots = small.tile([P, 2 * GROUP], F32)
-            nc.gpsimd.tensor_tensor(out=roots[:], in0=bases[:], in1=exponents[:], op=ALU.pow)
-            items[i]["inverse_nq"] = roots[:, 0:GROUP]
-            items[i]["ceiling"] = roots[:, GROUP : 2 * GROUP]
+            if not is_keys(i):
+                raised = small.tile([P, GROUP], F32)
+                nc.gpsimd.tensor_scalar(
+                    out=raised[:],
+                    in0=floored[:],
+                    scalar1=1.0 / EPS,
+                    scalar2=0.0,
+                    op0=ALU.mult,
+                    op1=ALU.add,
+                )
+                ceiling = small.tile([P, GROUP], F32)
+                nc.gpsimd.tensor_tensor(
+                    out=ceiling[:], in0=raised[:], in1=inverse[:], op=ALU.mult
+                )
+                items[i]["ceiling"] = ceiling
 
         def quantise(i):
             pool = key_keep if is_keys(i) else packed
@@ -153,14 +190,14 @@ def tile_attcosine_t_kernel(tc, query, y, out_0, out_1):
             items[i]["codes"] = codes
             items[i]["scales"] = scales
 
-        def spread_key_norms(i):
+        def spread_norms(i):
             bank = dot_banks.tile([P, GROUP, P], F32, tag="dots")
             for t in range(GROUP):
-                repeated = spread.tile([P, P], F32)
-                nc.vector.tensor_copy(
-                    out=repeated[:], in_=items[i]["inverse"][:, t : t + 1].to_broadcast([P, P])
+                nc.tensor.transpose(
+                    bank[:, t, :],
+                    items[i]["inverse"][:, t : t + 1].to_broadcast([P, P]),
+                    identity[:],
                 )
-                nc.tensor.transpose(bank[:, t, :], repeated[:], identity[:])
             items[i]["spread"] = bank
 
         def keep_keys(i):
@@ -175,119 +212,191 @@ def tile_attcosine_t_kernel(tc, query, y, out_0, out_1):
             side["inverse_ny"] = inverse_ny
             side["negative_shift"] = negative_shift
 
-        def multiply(i):
-            side = keys[items[i]["b"]]
-            banks = []
-            for t in range(GROUP):
-                dots = dot_banks.tile([P, LY], F32, tag="dots")
-                for k in range(PASSES):
-                    q_cols = slice((t * PASSES + k) * P, (t * PASSES + k + 1) * P)
-                    y_cols = slice(k * LY, (k + 1) * LY)
-                    nc.tensor.matmul_mx(
-                        out=dots[:],
-                        lhsT=items[i]["codes"][:, q_cols].bitcast(FP8X4),
-                        lhsT_scale=items[i]["scales"][:, q_cols],
-                        rhs=side["codes"][:, y_cols].bitcast(FP8X4),
-                        rhs_scale=side["scales"][:, y_cols],
-                        start=(k == 0),
-                        stop=(k == PASSES - 1),
-                    )
-                banks.append(dots)
-            items[i]["dots"] = banks
-
-        def scale(i):
-            side, g = keys[items[i]["b"]], items[i]["g"]
-            scaled = work.tile([P, GROUP, LY], F32)
-            for t in range(GROUP):
-                nc.vector.scalar_tensor_tensor(
-                    out=scaled[:, t, :],
-                    in0=side["inverse_ny"][:],
-                    scalar=items[i]["ceiling"][:, t : t + 1],
-                    in1=items[i]["dots"][t][:],
-                    op0=ALU.min,
-                    op1=ALU.mult,
+        def multiply(i, t):
+            side = items[i - 1 - items[i]["g"]]
+            dots = dot_banks.tile([P, LY], F32, tag="dots")
+            for k in range(PASSES):
+                q_cols = slice((t * PASSES + k) * P, (t * PASSES + k + 1) * P)
+                y_cols = slice(k * LY, (k + 1) * LY)
+                nc.tensor.matmul_mx(
+                    out=dots[:],
+                    lhsT=items[i]["codes"][:, q_cols].bitcast(FP8X4),
+                    lhsT_scale=items[i]["scales"][:, q_cols],
+                    rhs=side["codes"][:, y_cols].bitcast(FP8X4),
+                    rhs_scale=side["scales"][:, y_cols],
+                    start=(k == 0),
+                    stop=(k == PASSES - 1),
                 )
-            negative_top = small.tile([P, GROUP], F32)
+            items[i]["dots"][t] = dots
+
+        def scale(i, t):
+            side = keys[items[i]["b"]]
+            if t == 0:
+                items[i]["scaled"] = work.tile([P, GROUP, LY], F32, name="scaled")
+                items[i]["negative_top"] = small.tile([P, GROUP], F32, name="negative_top")
+            nc.vector.scalar_tensor_tensor(
+                out=items[i]["scaled"][:, t, :],
+                in0=side["inverse_ny"][:],
+                scalar=items[i]["ceiling"][:, t : t + 1],
+                in1=items[i]["dots"][t][:],
+                op0=ALU.min,
+                op1=ALU.mult,
+            )
+
+        def top(i, t0, t1):
             nc.vector.tensor_reduce(
-                out=negative_top[:],
-                in_=scaled[:],
+                out=items[i]["negative_top"][:, t0:t1],
+                in_=items[i]["scaled"][:, t0:t1, :],
                 axis=mybir.AxisListType.X,
                 op=ALU.max,
                 negate=True,
             )
-            nc.vector.tensor_mul(
-                out=side["negative_shift"][:, g * GROUP : (g + 1) * GROUP],
-                in0=negative_top[:],
-                in1=items[i]["inverse_nq"],
-            )
-            items[i]["scaled"] = scaled
 
-        def exponentials(i):
+        def shift(i, t0, t1, engine):
             side, g = keys[items[i]["b"]], items[i]["g"]
-            raised = work.tile([P, GROUP, LY], F32)
-            row_sums = small.tile([P, GROUP], F32)
-            for t in range(GROUP):
-                column = g * GROUP + t
-                nc.scalar.activation(
-                    out=raised[:, t, :],
-                    in_=items[i]["scaled"][:, t, :],
-                    func=ACT.Exp,
-                    bias=side["negative_shift"][:, column : column + 1],
-                    scale=items[i]["inverse_nq"][:, t : t + 1],
-                    accum_out=row_sums[:, t : t + 1],
-                )
-            items[i]["raised"] = raised
-            items[i]["row_sums"] = row_sums
+            engine.tensor_tensor(
+                out=side["negative_shift"][:, g * GROUP + t0 : g * GROUP + t1],
+                in0=items[i]["negative_top"][:, t0:t1],
+                in1=items[i]["inverse"][:, t0:t1],
+                op=ALU.mult,
+            )
 
-        def invert_row_sums(i):
-            inverse_sums = small.tile([P, GROUP], F32)
-            nc.vector.reciprocal(out=inverse_sums[:], in_=items[i]["row_sums"][:])
-            items[i]["inverse_sums"] = inverse_sums
+        def exponential(i, t):
+            side, g = keys[items[i]["b"]], items[i]["g"]
+            if t == 0:
+                items[i]["raised"] = work.tile([P, GROUP, LY], F32, name="raised")
+                items[i]["row_sums"] = small.tile([P, GROUP], F32, name="row_sums")
+                items[i]["inverse_sums"] = small.tile([P, GROUP], F32, name="inverse_sums")
+                items[i]["att"] = stores.tile([P, GROUP, LY], F32, name="att")
+            column = g * GROUP + t
+            nc.scalar.activation(
+                out=items[i]["raised"][:, t, :],
+                in_=items[i]["scaled"][:, t, :],
+                func=ACT.Exp,
+                bias=side["negative_shift"][:, column : column + 1],
+                scale=items[i]["inverse"][:, t : t + 1],
+                accum_out=items[i]["row_sums"][:, t : t + 1],
+            )
 
-        def finish(i):
+        def invert_row_sums(i, t0, t1):
+            nc.vector.reciprocal(
+                out=items[i]["inverse_sums"][:, t0:t1], in_=items[i]["row_sums"][:, t0:t1]
+            )
+
+        def normalise(i, t, engine):
+            engine.tensor_scalar(
+                out=items[i]["att"][:, t, :],
+                in0=items[i]["raised"][:, t, :],
+                scalar1=items[i]["inverse_sums"][:, t : t + 1],
+                scalar2=0.0,
+                op0=ALU.mult,
+                op1=ALU.add,
+            )
+
+        def store(i, t0, t1):
             b, g = items[i]["b"], items[i]["g"]
-            att = stores.tile([P, GROUP, LY], F32)
-            for t in range(GROUP):
-                nc.gpsimd.tensor_scalar(
-                    out=att[:, t, :],
-                    in0=items[i]["raised"][:, t, :],
-                    scalar1=items[i]["inverse_sums"][:, t : t + 1],
-                    scalar2=0.0,
-                    op0=ALU.mult,
-                    op1=ALU.add,
-                )
-            nc.sync.dma_start(out=att_view[b][:, g * GROUP : (g + 1) * GROUP, :], in_=att[:])
-            if g == GROUPS - 1:
-                sim = stores.tile([P, TILES], F32)
-                nc.vector.tensor_scalar_mul(
-                    out=sim[:], in0=keys[b]["negative_shift"][:], scalar1=-1.0
-                )
-                nc.sync.dma_start(out=sim_view[b], in_=sim[:])
+            nc.sync.dma_start(
+                out=att_view[b][:, g * GROUP + t0 : g * GROUP + t1, :],
+                in_=items[i]["att"][:, t0:t1, :],
+            )
 
-        for s in range(-3, len(items) + 5):
-            if is_keys(s + 3) or is_queries(s + 3):
-                load(s + 3)
-            if is_keys(s - 1) or is_queries(s - 1):
-                regroup(s - 1)
-            if is_keys(s) or is_queries(s):
-                turn(s)
-            if is_queries(s - 5):
-                invert_row_sums(s - 5)
-            if is_keys(s - 2) or is_queries(s - 2):
-                quantise(s - 2)
-            if is_keys(s - 3):
-                keep_keys(s - 3)
-            if is_queries(s - 3):
-                scale(s - 3)
-            if is_keys(s - 2):
-                spread_key_norms(s - 2)
-            if is_queries(s - 2):
-                multiply(s - 2)
-            if is_queries(s - 4):
-                exponentials(s - 4)
-            if is_queries(s - 5):
-                finish(s - 5)
-            if is_keys(s - 1):
-                key_norms(s - 1)
-            if is_queries(s - 1):
-                query_norms(s - 1)
+        def store_top(i):
+            b = items[i]["b"]
+            sim = stores.tile([P, TILES], F32)
+            nc.scalar.mul(sim[:], keys[b]["negative_shift"][:], -1.0)
+            nc.sync.dma_start(out=sim_view[b], in_=sim[:])
+
+        def group_at(n, offset):
+            i, t = divmod(n - offset, GROUP)
+            return i if t == 0 and 0 <= i <= last else None
+
+        def tile_at(n, offset):
+            i, t = divmod(n - offset, GROUP)
+            return (i, t) if 0 <= i <= last else None
+
+        def exp_at(i):
+            return 17 if i < last - 1 else 14
+
+        def finish_at(i):
+            return 22 if i < last - 1 else 18
+
+        def tiles_at(n, offset):
+            pairs = []
+            for i in range(len(items)):
+                t = n - GROUP * i - (offset if isinstance(offset, int) else offset(i))
+                if 0 <= t < GROUP:
+                    pairs.append((i, t))
+            return pairs
+
+        for n in range(-12, GROUP * len(items) + 28):
+            i = group_at(n, -12)
+            if i is not None:
+                load(i)
+            for i, t in tiles_at(n, 8):
+                if not is_keys(i):
+                    multiply(i, t)
+            for i, t in tiles_at(n, 3):
+                if on_tensor(i, t):
+                    gram(i, t)
+            for i, t in tiles_at(n, 0):
+                turn(i, t)
+            for i, t in tiles_at(n, 2):
+                regroup(i, t)
+            for i, t in tiles_at(n, exp_at):
+                if not is_keys(i):
+                    exponential(i, t)
+            for i, t in tiles_at(n, 0):
+                if not on_tensor(i, t):
+                    square(i, t)
+            for i, t in tiles_at(n, 10):
+                if not is_keys(i):
+                    scale(i, t)
+            i = group_at(n, 6)
+            if i is not None:
+                quantise(i)
+            i = group_at(n, 7)
+            if i is not None and not is_keys(i):
+                diagonal(i)
+                norms(i)
+            for i, t in tiles_at(n, finish_at):
+                if not is_keys(i):
+                    if i < last - 1:
+                        if t == 0:
+                            invert_row_sums(i, 0, GROUP)
+                    else:
+                        invert_row_sums(i, t, t + 1)
+                        normalise(i, t, nc.vector)
+            i = group_at(n, 4)
+            if i is not None and is_keys(i):
+                norms(i)
+            i = group_at(n, 8)
+            if i is not None and is_keys(i):
+                spread_norms(i)
+            i = group_at(n, 10)
+            if i is not None and is_keys(i):
+                keep_keys(i)
+            for i, t in tiles_at(n, 12):
+                if not is_keys(i):
+                    if i == last:
+                        pass
+                    elif (t + 1) % 2 == 0:
+                        shift(i, t + 1 - 2, t + 1, nc.gpsimd)
+            for i, t in tiles_at(n, 11):
+                if not is_keys(i):
+                    if i == last:
+                        top(i, t, t + 1)
+                        shift(i, t, t + 1, nc.gpsimd)
+                    elif (t + 1) % 2 == 0:
+                        top(i, t + 1 - 2, t + 1)
+            for i, t in tiles_at(n, finish_at):
+                if not is_keys(i):
+                    if i < last - 1:
+                        normalise(i, t, nc.gpsimd)
+                    if i < last - 2:
+                        if t == GROUP - 1:
+                            store(i, 0, GROUP)
+                    else:
+                        store(i, t, t + 1)
+            i = group_at(n, 16)
+            if i is not None and not is_keys(i) and items[i]["g"] == GROUPS - 1:
+                store_top(i)

@@ -332,6 +332,9 @@ def tile_attcosine_t_kernel(tc, query, y, out_0, out_1):
             i = group_at(n, -12)
             if i is not None:
                 load(i)
+            i = group_at(n, 6)
+            if i is not None and not is_keys(i):
+                diagonal(i)
             for i, t in tiles_at(n, 8):
                 if not is_keys(i):
                     multiply(i, t)
@@ -356,7 +359,6 @@ def tile_attcosine_t_kernel(tc, query, y, out_0, out_1):
                 quantise(i)
             i = group_at(n, 7)
             if i is not None and not is_keys(i):
-                diagonal(i)
                 norms(i)
             for i, t in tiles_at(n, finish_at):
                 if not is_keys(i):

@@ -23,7 +23,7 @@ HALVES = 2
 BLOCKS = PASSES * HALVES
 GROUP = 4
 TILES = LQ // P
-EARLY, SHARE, LATE = 12, 7, 66
+EARLY, SHARE, LATE = 12, 8, 66
 GROUPS = TILES // GROUP
 WORDS = GROUP * PASSES * P
 
@@ -63,7 +63,7 @@ def tile_attcosine_t_kernel(tc, query, y, out_0, out_1):
         packed = ctx.enter_context(tc.tile_pool(name="packed", bufs=3))
         small = ctx.enter_context(tc.tile_pool(name="small", bufs=8))
         work = ctx.enter_context(tc.tile_pool(name="work", bufs=4))
-        stores = ctx.enter_context(tc.tile_pool(name="stores", bufs=5))
+        stores = ctx.enter_context(tc.tile_pool(name="stores", bufs=4))
         turn_banks = ctx.enter_context(tc.psum_pool(name="turn_banks", bufs=3))
         gram_banks = ctx.enter_context(tc.psum_pool(name="gram_banks", bufs=1))
         dot_banks = ctx.enter_context(tc.psum_pool(name="dot_banks", bufs=GROUP))
@@ -315,10 +315,10 @@ def tile_attcosine_t_kernel(tc, query, y, out_0, out_1):
             return (i, t) if 0 <= i <= last else None
 
         def exp_at(i):
-            return 17 if i < last - 1 else 14
+            return 16 if i < last - 1 else 14
 
         def finish_at(i):
-            return 22 if i < last - 1 else 18
+            return 19 if i < last - 1 else 17
 
         def tiles_at(n, offset):
             pairs = []
@@ -362,12 +362,14 @@ def tile_attcosine_t_kernel(tc, query, y, out_0, out_1):
                 norms(i)
             for i, t in tiles_at(n, finish_at):
                 if not is_keys(i):
-                    if i < last - 1:
-                        if t == 0:
-                            invert_row_sums(i, 0, GROUP)
+                    normalise(i, t, nc.vector)
+            for i, t in tiles_at(n, finish_at):
+                if not is_keys(i):
+                    if i < last - 2:
+                        if t == GROUP - 1:
+                            store(i, 0, GROUP)
                     else:
-                        invert_row_sums(i, t, t + 1)
-                        normalise(i, t, nc.vector)
+                        store(i, t, t + 1)
             i = group_at(n, 4)
             if i is not None and is_keys(i):
                 norms(i)
@@ -390,15 +392,13 @@ def tile_attcosine_t_kernel(tc, query, y, out_0, out_1):
                         shift(i, t, t + 1, nc.gpsimd)
                     elif (t + 1) % 2 == 0:
                         top(i, t + 1 - 2, t + 1)
-            for i, t in tiles_at(n, finish_at):
+            for i, t in tiles_at(n, lambda i: finish_at(i) - 2):
                 if not is_keys(i):
                     if i < last - 1:
-                        normalise(i, t, nc.gpsimd)
-                    if i < last - 2:
-                        if t == GROUP - 1:
-                            store(i, 0, GROUP)
+                        if (t + 1) % 2 == 0:
+                            invert_row_sums(i, t + 1 - 2, t + 1)
                     else:
-                        store(i, t, t + 1)
+                        invert_row_sums(i, t, t + 1)
             i = group_at(n, 16)
             if i is not None and not is_keys(i) and items[i]["g"] == GROUPS - 1:
                 store_top(i)

@@ -39,11 +39,9 @@ def tile_attcosine_t_kernel(tc, query, y, out_0, out_1):
     sim_view = [out_1[b, 0].rearrange("(p s) -> p s", s=TILES) for b in range(B)]
     y_view = [y[b].rearrange("(t p) d -> p t d", p=P) for b in range(B)]
 
-    items = []
-    for b in range(B):
-        items.append({"b": b, "g": None})
-        for g in range(GROUPS):
-            items.append({"b": b, "g": g})
+    items = [{"b": b, "g": g} for b in range(B) for g in range(GROUPS)]
+    items.insert(0, {"b": 0, "g": None})
+    items.insert(1, {"b": 1, "g": None})
     last = len(items) - 1
     keys = [{} for b in range(B)]
 
@@ -63,7 +61,7 @@ def tile_attcosine_t_kernel(tc, query, y, out_0, out_1):
         packed = ctx.enter_context(tc.tile_pool(name="packed", bufs=3))
         small = ctx.enter_context(tc.tile_pool(name="small", bufs=8))
         work = ctx.enter_context(tc.tile_pool(name="work", bufs=4))
-        stores = ctx.enter_context(tc.tile_pool(name="stores", bufs=4))
+        stores = ctx.enter_context(tc.tile_pool(name="stores", bufs=5))
         turn_banks = ctx.enter_context(tc.psum_pool(name="turn_banks", bufs=3))
         gram_banks = ctx.enter_context(tc.psum_pool(name="gram_banks", bufs=1))
         dot_banks = ctx.enter_context(tc.psum_pool(name="dot_banks", bufs=GROUP))
@@ -180,15 +178,18 @@ def tile_attcosine_t_kernel(tc, query, y, out_0, out_1):
                 )
                 items[i]["ceiling"] = ceiling
 
-        def quantise(i):
-            pool = key_keep if is_keys(i) else packed
-            codes = pool.tile([P, WORDS], U32, align_bytes=64)
-            scales = pool.tile([P, WORDS], U8, align_bytes=64)
+        def quantise(i, t0, t1):
+            owner = keys[items[i]["b"]] if is_keys(i) else items[i]
+            if t0 == 0:
+                pool = key_keep if is_keys(i) else packed
+                owner["codes"] = pool.tile([P, WORDS], U32, align_bytes=64, name="codes")
+                owner["scales"] = pool.tile([P, WORDS], U8, align_bytes=64, name="scales")
+            cols = slice(t0 * PASSES * P, t1 * PASSES * P)
             nc.vector.quantize_mx(
-                out=codes[:].bitcast(FP8X4), scales=scales[:], in_=items[i]["grouped"][:]
+                out=owner["codes"][:, cols].bitcast(FP8X4),
+                scales=owner["scales"][:, cols],
+                in_=items[i]["grouped"][:, t0 * PASSES * P * PACK : t1 * PASSES * P * PACK],
             )
-            items[i]["codes"] = codes
-            items[i]["scales"] = scales
 
         def spread_norms(i):
             bank = dot_banks.tile([P, GROUP, P], F32, tag="dots")
@@ -207,13 +208,11 @@ def tile_attcosine_t_kernel(tc, query, y, out_0, out_1):
             )
             negative_shift = key_keep.tile([P, TILES], F32)
             side = keys[items[i]["b"]]
-            side["codes"] = items[i]["codes"]
-            side["scales"] = items[i]["scales"]
             side["inverse_ny"] = inverse_ny
             side["negative_shift"] = negative_shift
 
         def multiply(i, t):
-            side = items[i - 1 - items[i]["g"]]
+            side = keys[items[i]["b"]]
             dots = dot_banks.tile([P, LY], F32, tag="dots")
             for k in range(PASSES):
                 q_cols = slice((t * PASSES + k) * P, (t * PASSES + k + 1) * P)
@@ -283,6 +282,14 @@ def tile_attcosine_t_kernel(tc, query, y, out_0, out_1):
                 out=items[i]["inverse_sums"][:, t0:t1], in_=items[i]["row_sums"][:, t0:t1]
             )
 
+        def normalise_on_scalar(i, t):
+            nc.scalar.activation(
+                out=items[i]["att"][:, t, :],
+                in_=items[i]["raised"][:, t, :],
+                func=ACT.Copy,
+                scale=items[i]["inverse_sums"][:, t : t + 1],
+            )
+
         def normalise(i, t, engine):
             engine.tensor_scalar(
                 out=items[i]["att"][:, t, :],
@@ -315,10 +322,13 @@ def tile_attcosine_t_kernel(tc, query, y, out_0, out_1):
             return (i, t) if 0 <= i <= last else None
 
         def exp_at(i):
-            return 16 if i < last - 1 else 14
+            return 16 if i < last - 2 else 13
 
         def finish_at(i):
-            return 19 if i < last - 1 else 17
+            return 19 if i < last - 2 else 16
+
+        def on_gpsimd(i, t):
+            return t % 2 == 1
 
         def tiles_at(n, offset):
             pairs = []
@@ -354,22 +364,42 @@ def tile_attcosine_t_kernel(tc, query, y, out_0, out_1):
             for i, t in tiles_at(n, 10):
                 if not is_keys(i):
                     scale(i, t)
-            i = group_at(n, 6)
-            if i is not None:
-                quantise(i)
-            i = group_at(n, 7)
-            if i is not None and not is_keys(i):
-                norms(i)
-            for i, t in tiles_at(n, finish_at):
-                if not is_keys(i):
-                    normalise(i, t, nc.vector)
-            for i, t in tiles_at(n, finish_at):
+            for i, t in tiles_at(n, 3):
+                if is_keys(i):
+                    if t == GROUP - 1:
+                        quantise(i, 0, GROUP)
+                elif (t + 1) % 4 == 0:
+                    quantise(i, t + 1 - 4, t + 1)
+            for i, t in tiles_at(n, lambda i: finish_at(i) - 2):
                 if not is_keys(i):
                     if i < last - 2:
-                        if t == GROUP - 1:
-                            store(i, 0, GROUP)
-                    else:
-                        store(i, t, t + 1)
+                        if (t + 1) % 2 == 0:
+                            invert_row_sums(i, t + 1 - 2, t + 1)
+            for i, t in tiles_at(n, 11):
+                if not is_keys(i):
+                    if i >= last - 2:
+                        top(i, t, t + 1)
+                        shift(i, t, t + 1, nc.gpsimd)
+                    elif (t + 1) % 2 == 0:
+                        top(i, t + 1 - 2, t + 1)
+            for i, t in tiles_at(n, finish_at):
+                if not is_keys(i):
+                    if i >= last - 2:
+                        invert_row_sums(i, t, t + 1)
+                        if False:
+                            normalise_on_scalar(i, t)
+                        elif False:
+                            normalise(i, t, nc.gpsimd)
+                        else:
+                            normalise(i, t, nc.vector)
+                    elif not on_gpsimd(i, t):
+                        normalise(i, t, nc.vector)
+            i = group_at(n, 14)
+            if i is not None and not is_keys(i) and i < last - 2:
+                shift(i, 0, GROUP, nc.gpsimd)
+            i = group_at(n, 6)
+            if i is not None and not is_keys(i):
+                norms(i)
             i = group_at(n, 4)
             if i is not None and is_keys(i):
                 norms(i)
@@ -379,26 +409,15 @@ def tile_attcosine_t_kernel(tc, query, y, out_0, out_1):
             i = group_at(n, 10)
             if i is not None and is_keys(i):
                 keep_keys(i)
-            for i, t in tiles_at(n, 12):
+            for i, t in tiles_at(n, finish_at):
                 if not is_keys(i):
-                    if i == last:
-                        pass
-                    elif (t + 1) % 2 == 0:
-                        shift(i, t + 1 - 2, t + 1, nc.gpsimd)
-            for i, t in tiles_at(n, 11):
-                if not is_keys(i):
-                    if i == last:
-                        top(i, t, t + 1)
-                        shift(i, t, t + 1, nc.gpsimd)
-                    elif (t + 1) % 2 == 0:
-                        top(i, t + 1 - 2, t + 1)
-            for i, t in tiles_at(n, lambda i: finish_at(i) - 2):
-                if not is_keys(i):
-                    if i < last - 1:
-                        if (t + 1) % 2 == 0:
-                            invert_row_sums(i, t + 1 - 2, t + 1)
+                    if i < last - 2 and on_gpsimd(i, t):
+                        normalise(i, t, nc.gpsimd)
+                    if i < last - 3:
+                        if t == GROUP - 1:
+                            store(i, 0, GROUP)
                     else:
-                        invert_row_sums(i, t, t + 1)
-            i = group_at(n, 16)
+                        store(i, t, t + 1)
+            i = group_at(n, 18)
             if i is not None and not is_keys(i) and items[i]["g"] == GROUPS - 1:
                 store_top(i)

@@ -51,7 +51,7 @@ def tile_attcosine_t_kernel(tc, query, y, out_0, out_1):
     def on_tensor(i, t):
         if is_keys(i):
             return False
-        return t == 0 or (t == 2 and items[i]["g"] % 2 == 0)
+        return t == 0 or (t == 1 and items[i]["g"] % 2 == 0)
 
     with ExitStack() as ctx:
         consts = ctx.enter_context(tc.tile_pool(name="consts", bufs=1))
@@ -123,22 +123,29 @@ def tile_attcosine_t_kernel(tc, query, y, out_0, out_1):
                 accum_out=items[i]["sums"][:, t : t + 1],
             )
 
-        def gram(i, t):
+        def gram(i, part):
             values = items[i]["grouped"][:].rearrange(
                 grouped_order(i).replace("u", "w"), t=GROUP, k=PASSES, w=PACK
             )
-            if t == 0:
+            if part == 0:
                 items[i]["gram"] = gram_banks.tile([P, GROUP, P], F32, name="gram")
-            for k in range(PASSES):
-                for w in range(PACK):
-                    x = values[:, t, k, :, w]
-                    nc.tensor.matmul(
-                        items[i]["gram"][:, t, :],
-                        lhsT=x,
-                        rhs=x,
-                        start=(k == 0 and w == 0),
-                        stop=(k == PASSES - 1 and w == PACK - 1),
-                    )
+            pieces = [
+                (t, k, w)
+                for t in range(GROUP)
+                if on_tensor(i, t)
+                for k in range(PASSES)
+                for w in range(PACK)
+            ]
+            count = len(pieces)
+            for t, k, w in pieces[count * part // 3 : count * (part + 1) // 3]:
+                x = values[:, t, k, :, w]
+                nc.tensor.matmul(
+                    items[i]["gram"][:, t, :],
+                    lhsT=x,
+                    rhs=x,
+                    start=(k == 0 and w == 0),
+                    stop=(k == PASSES - 1 and w == PACK - 1),
+                )
 
         def diagonal(i):
             for t in range(GROUP):
@@ -300,9 +307,9 @@ def tile_attcosine_t_kernel(tc, query, y, out_0, out_1):
                 op1=ALU.add,
             )
 
-        def store(i, t0, t1):
+        def store(i, t0, t1, engine=nc.sync):
             b, g = items[i]["b"], items[i]["g"]
-            nc.sync.dma_start(
+            engine.dma_start(
                 out=att_view[b][:, g * GROUP + t0 : g * GROUP + t1, :],
                 in_=items[i]["att"][:, t0:t1, :],
             )
@@ -330,6 +337,9 @@ def tile_attcosine_t_kernel(tc, query, y, out_0, out_1):
         def on_gpsimd(i, t):
             return t % 2 == 1
 
+        def on_scalar(i, t):
+            return i >= last - 2 and (i < last)
+
         def tiles_at(n, offset):
             pairs = []
             for i in range(len(items)):
@@ -349,7 +359,7 @@ def tile_attcosine_t_kernel(tc, query, y, out_0, out_1):
                 if not is_keys(i):
                     multiply(i, t)
             for i, t in tiles_at(n, 3):
-                if on_tensor(i, t):
+                if not is_keys(i) and t < 3:
                     gram(i, t)
             for i, t in tiles_at(n, 0):
                 turn(i, t)
@@ -358,6 +368,10 @@ def tile_attcosine_t_kernel(tc, query, y, out_0, out_1):
             for i, t in tiles_at(n, exp_at):
                 if not is_keys(i):
                     exponential(i, t)
+            for i, t in tiles_at(n, lambda i: finish_at(i) + 1):
+                if not is_keys(i) and on_scalar(i, t):
+                    normalise_on_scalar(i, t)
+                    store(i, t, t + 1, nc.scalar)
             for i, t in tiles_at(n, 0):
                 if not on_tensor(i, t):
                     square(i, t)
@@ -386,11 +400,7 @@ def tile_attcosine_t_kernel(tc, query, y, out_0, out_1):
                 if not is_keys(i):
                     if i >= last - 2:
                         invert_row_sums(i, t, t + 1)
-                        if False:
-                            normalise_on_scalar(i, t)
-                        elif False:
-                            normalise(i, t, nc.gpsimd)
-                        else:
+                        if not on_scalar(i, t):
                             normalise(i, t, nc.vector)
                     elif not on_gpsimd(i, t):
                         normalise(i, t, nc.vector)
@@ -413,10 +423,10 @@ def tile_attcosine_t_kernel(tc, query, y, out_0, out_1):
                 if not is_keys(i):
                     if i < last - 2 and on_gpsimd(i, t):
                         normalise(i, t, nc.gpsimd)
-                    if i < last - 3:
+                    if i < last - 2:
                         if t == GROUP - 1:
                             store(i, 0, GROUP)
-                    else:
+                    elif not on_scalar(i, t):
                         store(i, t, t + 1)
             i = group_at(n, 18)
             if i is not None and not is_keys(i) and items[i]["g"] == GROUPS - 1:

@@ -335,10 +335,10 @@ def tile_attcosine_t_kernel(tc, query, y, out_0, out_1):
             return 19 if i < last - 2 else 16
 
         def on_gpsimd(i, t):
-            return t % 2 == 1
+            return t > 0
 
         def on_scalar(i, t):
-            return i >= last - 2 and (i < last)
+            return i >= last - 2 and (False)
 
         def tiles_at(n, offset):
             pairs = []

@@ -23,7 +23,7 @@ HALVES = 2
 BLOCKS = PASSES * HALVES
 GROUP = 4
 TILES = LQ // P
-EARLY, SHARE, LATE = 12, 8, 66
+EARLY, SHARE, LATE = 12, 7, 66
 GROUPS = TILES // GROUP
 WORDS = GROUP * PASSES * P
 
@@ -335,7 +335,7 @@ def tile_attcosine_t_kernel(tc, query, y, out_0, out_1):
             return 19 if i < last - 2 else 16
 
         def on_gpsimd(i, t):
-            return t > 0
+            return True
 
         def on_scalar(i, t):
             return i >= last - 2 and (False)
@@ -352,9 +352,6 @@ def tile_attcosine_t_kernel(tc, query, y, out_0, out_1):
             i = group_at(n, -12)
             if i is not None:
                 load(i)
-            i = group_at(n, 6)
-            if i is not None and not is_keys(i):
-                diagonal(i)
             for i, t in tiles_at(n, 8):
                 if not is_keys(i):
                     multiply(i, t)
@@ -384,6 +381,9 @@ def tile_attcosine_t_kernel(tc, query, y, out_0, out_1):
                         quantise(i, 0, GROUP)
                 elif (t + 1) % 4 == 0:
                     quantise(i, t + 1 - 4, t + 1)
+            i = group_at(n, 6)
+            if i is not None and not is_keys(i):
+                diagonal(i)
             for i, t in tiles_at(n, lambda i: finish_at(i) - 2):
                 if not is_keys(i):
                     if i < last - 2:

from contextlib import ExitStack

import concourse.mybir as mybir
from concourse.masks import make_identity

F32 = mybir.dt.float32
BF16 = mybir.dt.bfloat16
U32 = mybir.dt.uint32
U8 = mybir.dt.uint8
FP8X4 = mybir.dt.float8_e4m3fn_x4
ALU = mybir.AluOpType
ACT = mybir.ActivationFunctionType

B, LQ, LY, D = 2, 4096, 512, 1024
EPS = 1e-8
TINY = 1e-36

P = 128
PACK = 4
K_PASS = P * PACK
PASSES = D // K_PASS
HALVES = 2
BLOCKS = PASSES * HALVES
GROUP = 4
TILES = LQ // P
EARLY, SHARE, LATE = 12, 7, 66
GROUPS = TILES // GROUP
WORDS = GROUP * PASSES * P

FLOPS = 2 * B * LQ * LY * D


def tile_attcosine_t_kernel(tc, query, y, out_0, out_1):
    nc = tc.nc
    assert LY == GROUP * P

    q_view = [query[b].rearrange("(p s) d -> p s d", s=TILES) for b in range(B)]
    att_view = [out_0[b].rearrange("(p s) j -> p s j", s=TILES) for b in range(B)]
    sim_view = [out_1[b, 0].rearrange("(p s) -> p s", s=TILES) for b in range(B)]
    y_view = [y[b].rearrange("(t p) d -> p t d", p=P) for b in range(B)]

    items = [{"b": b, "g": g} for b in range(B) for g in range(GROUPS)]
    items.insert(0, {"b": 0, "g": None})
    items.insert(1, {"b": 1, "g": None})
    last = len(items) - 1
    keys = [{} for b in range(B)]

    def is_keys(i):
        return items[i]["g"] is None

    def on_tensor(i, t):
        if is_keys(i):
            return False
        return t == 0 or (t == 1 and items[i]["g"] % 2 == 0)

    with ExitStack() as ctx:
        consts = ctx.enter_context(tc.tile_pool(name="consts", bufs=1))
        key_keep = ctx.enter_context(tc.tile_pool(name="key_keep", bufs=B))
        loads = ctx.enter_context(tc.tile_pool(name="loads", bufs=5))
        squares = ctx.enter_context(tc.tile_pool(name="squares", bufs=4))
        packed = ctx.enter_context(tc.tile_pool(name="packed", bufs=3))
        small = ctx.enter_context(tc.tile_pool(name="small", bufs=8))
        work = ctx.enter_context(tc.tile_pool(name="work", bufs=4))
        stores = ctx.enter_context(tc.tile_pool(name="stores", bufs=5))
        turn_banks = ctx.enter_context(tc.psum_pool(name="turn_banks", bufs=3))
        gram_banks = ctx.enter_context(tc.psum_pool(name="gram_banks", bufs=1))
        dot_banks = ctx.enter_context(tc.psum_pool(name="dot_banks", bufs=GROUP))
        ctx.enter_context(tc.manual_schedule())

        identity = consts.tile([P, P], F32)
        make_identity(nc, identity[:])
        exponents = consts.tile([P, GROUP], F32)
        nc.gpsimd.memset(exponents[:], -0.5)

        def load(i):
            b, g = items[i]["b"], items[i]["g"]
            rows = loads.tile([P, GROUP, D], BF16)
            if i == 0:
                for t in range(GROUP):
                    nc.sync.dma_start(out=rows[:, t, :], in_=y_view[b][:, t, :])
            elif g is None:
                nc.sync.dma_start(out=rows[:], in_=y_view[b])
            else:
                nc.sync.dma_start(out=rows[:], in_=q_view[b][:, g * GROUP : (g + 1) * GROUP, :])
            sums = small.tile([P, GROUP], F32)
            items[i]["rows"] = rows
            items[i]["sums"] = sums
            items[i]["banks"] = {}
            items[i]["dots"] = {}

        def turn(i, t):
            words = items[i]["rows"][:, t, :].bitcast(F32)
            bank = turn_banks.tile([P, BLOCKS, P], F32)
            for c in range(BLOCKS):
                nc.tensor.transpose(bank[:, c, :], words[:, c * P : (c + 1) * P], identity[:])
            items[i]["banks"][t] = bank

        def grouped_order(i):
            return "p (k t r u) -> p t k r u" if is_keys(i) else "p (t k r u) -> p t k r u"

        def regroup(i, t):
            if t == 0:
                items[i]["grouped"] = packed.tile(
                    [P, WORDS * PACK], BF16, align_bytes=64, name="grouped"
                )
            grouped_words = items[i]["grouped"][:].bitcast(F32).rearrange(
                grouped_order(i), t=GROUP, k=PASSES, u=HALVES
            )
            n = GROUP * i + t
            on_scalar = n >= EARLY and (n * SHARE) % 8 < SHARE or n >= LATE
            copy = nc.scalar.copy if on_scalar else nc.vector.tensor_copy
            copy(
                out=grouped_words[:, t],
                in_=items[i]["banks"][t][:].rearrange("p (k u) r -> p k r u", u=HALVES),
            )

        def square(i, t):
            squared = squares.tile([P, D], BF16)
            nc.scalar.activation(
                out=squared[:],
                in_=items[i]["rows"][:, t, :],
                func=ACT.Square,
                accum_out=items[i]["sums"][:, t : t + 1],
            )

        def gram(i, part):
            values = items[i]["grouped"][:].rearrange(
                grouped_order(i).replace("u", "w"), t=GROUP, k=PASSES, w=PACK
            )
            if part == 0:
                items[i]["gram"] = gram_banks.tile([P, GROUP, P], F32, name="gram")
            pieces = [
                (t, k, w)
                for t in range(GROUP)
                if on_tensor(i, t)
                for k in range(PASSES)
                for w in range(PACK)
            ]
            count = len(pieces)
            for t, k, w in pieces[count * part // 3 : count * (part + 1) // 3]:
                x = values[:, t, k, :, w]
                nc.tensor.matmul(
                    items[i]["gram"][:, t, :],
                    lhsT=x,
                    rhs=x,
                    start=(k == 0 and w == 0),
                    stop=(k == PASSES - 1 and w == PACK - 1),
                )

        def diagonal(i):
            for t in range(GROUP):
                if on_tensor(i, t):
                    masked = squares.tile([P, P], F32)
                    nc.vector.scalar_tensor_tensor(
                        out=masked[:],
                        in0=items[i]["gram"][:, t, :],
                        scalar=1.0,
                        in1=identity[:],
                        op0=ALU.mult,
                        op1=ALU.mult,
                        accum_out=items[i]["sums"][:, t : t + 1],
                    )

        def norms(i):
            floored = small.tile([P, GROUP], F32)
            nc.gpsimd.tensor_scalar_max(out=floored[:], in0=items[i]["sums"][:], scalar1=TINY)
            inverse = small.tile([P, GROUP], F32)
            nc.gpsimd.tensor_tensor(
                out=inverse[:], in0=floored[:], in1=exponents[:], op=ALU.pow
            )
            items[i]["inverse"] = inverse
            if not is_keys(i):
                raised = small.tile([P, GROUP], F32)
                nc.gpsimd.tensor_scalar(
                    out=raised[:],
                    in0=floored[:],
                    scalar1=1.0 / EPS,
                    scalar2=0.0,
                    op0=ALU.mult,
                    op1=ALU.add,
                )
                ceiling = small.tile([P, GROUP], F32)
                nc.gpsimd.tensor_tensor(
                    out=ceiling[:], in0=raised[:], in1=inverse[:], op=ALU.mult
                )
                items[i]["ceiling"] = ceiling

        def quantise(i, t0, t1):
            owner = keys[items[i]["b"]] if is_keys(i) else items[i]
            if t0 == 0:
                pool = key_keep if is_keys(i) else packed
                owner["codes"] = pool.tile([P, WORDS], U32, align_bytes=64, name="codes")
                owner["scales"] = pool.tile([P, WORDS], U8, align_bytes=64, name="scales")
            cols = slice(t0 * PASSES * P, t1 * PASSES * P)
            nc.vector.quantize_mx(
                out=owner["codes"][:, cols].bitcast(FP8X4),
                scales=owner["scales"][:, cols],
                in_=items[i]["grouped"][:, t0 * PASSES * P * PACK : t1 * PASSES * P * PACK],
            )

        def spread_norms(i):
            bank = dot_banks.tile([P, GROUP, P], F32, tag="dots")
            for t in range(GROUP):
                nc.tensor.transpose(
                    bank[:, t, :],
                    items[i]["inverse"][:, t : t + 1].to_broadcast([P, P]),
                    identity[:],
                )
            items[i]["spread"] = bank

        def keep_keys(i):
            inverse_ny = key_keep.tile([P, LY], F32)
            nc.vector.tensor_copy(
                out=inverse_ny[:], in_=items[i]["spread"][:].rearrange("p t j -> p (t j)")
            )
            negative_shift = key_keep.tile([P, TILES], F32)
            side = keys[items[i]["b"]]
            side["inverse_ny"] = inverse_ny
            side["negative_shift"] = negative_shift

        def multiply(i, t):
            side = keys[items[i]["b"]]
            dots = dot_banks.tile([P, LY], F32, tag="dots")
            for k in range(PASSES):
                q_cols = slice((t * PASSES + k) * P, (t * PASSES + k + 1) * P)
                y_cols = slice(k * LY, (k + 1) * LY)
                nc.tensor.matmul_mx(
                    out=dots[:],
                    lhsT=items[i]["codes"][:, q_cols].bitcast(FP8X4),
                    lhsT_scale=items[i]["scales"][:, q_cols],
                    rhs=side["codes"][:, y_cols].bitcast(FP8X4),
                    rhs_scale=side["scales"][:, y_cols],
                    start=(k == 0),
                    stop=(k == PASSES - 1),
                )
            items[i]["dots"][t] = dots

        def scale(i, t):
            side = keys[items[i]["b"]]
            if t == 0:
                items[i]["scaled"] = work.tile([P, GROUP, LY], F32, name="scaled")
                items[i]["negative_top"] = small.tile([P, GROUP], F32, name="negative_top")
            nc.vector.scalar_tensor_tensor(
                out=items[i]["scaled"][:, t, :],
                in0=side["inverse_ny"][:],
                scalar=items[i]["ceiling"][:, t : t + 1],
                in1=items[i]["dots"][t][:],
                op0=ALU.min,
                op1=ALU.mult,
            )

        def top(i, t0, t1):
            nc.vector.tensor_reduce(
                out=items[i]["negative_top"][:, t0:t1],
                in_=items[i]["scaled"][:, t0:t1, :],
                axis=mybir.AxisListType.X,
                op=ALU.max,
                negate=True,
            )

        def shift(i, t0, t1, engine):
            side, g = keys[items[i]["b"]], items[i]["g"]
            engine.tensor_tensor(
                out=side["negative_shift"][:, g * GROUP + t0 : g * GROUP + t1],
                in0=items[i]["negative_top"][:, t0:t1],
                in1=items[i]["inverse"][:, t0:t1],
                op=ALU.mult,
            )

        def exponential(i, t):
            side, g = keys[items[i]["b"]], items[i]["g"]
            if t == 0:
                items[i]["raised"] = work.tile([P, GROUP, LY], F32, name="raised")
                items[i]["row_sums"] = small.tile([P, GROUP], F32, name="row_sums")
                items[i]["inverse_sums"] = small.tile([P, GROUP], F32, name="inverse_sums")
                items[i]["att"] = stores.tile([P, GROUP, LY], F32, name="att")
            column = g * GROUP + t
            nc.scalar.activation(
                out=items[i]["raised"][:, t, :],
                in_=items[i]["scaled"][:, t, :],
                func=ACT.Exp,
                bias=side["negative_shift"][:, column : column + 1],
                scale=items[i]["inverse"][:, t : t + 1],
                accum_out=items[i]["row_sums"][:, t : t + 1],
            )

        def invert_row_sums(i, t0, t1):
            nc.vector.reciprocal(
                out=items[i]["inverse_sums"][:, t0:t1], in_=items[i]["row_sums"][:, t0:t1]
            )

        def normalise_on_scalar(i, t):
            nc.scalar.activation(
                out=items[i]["att"][:, t, :],
                in_=items[i]["raised"][:, t, :],
                func=ACT.Copy,
                scale=items[i]["inverse_sums"][:, t : t + 1],
            )

        def normalise(i, t, engine):
            engine.tensor_scalar(
                out=items[i]["att"][:, t, :],
                in0=items[i]["raised"][:, t, :],
                scalar1=items[i]["inverse_sums"][:, t : t + 1],
                scalar2=0.0,
                op0=ALU.mult,
                op1=ALU.add,
            )

        def store(i, t0, t1, engine=nc.sync):
            b, g = items[i]["b"], items[i]["g"]
            engine.dma_start(
                out=att_view[b][:, g * GROUP + t0 : g * GROUP + t1, :],
                in_=items[i]["att"][:, t0:t1, :],
            )

        def store_top(i):
            b = items[i]["b"]
            sim = stores.tile([P, TILES], F32)
            nc.scalar.mul(sim[:], keys[b]["negative_shift"][:], -1.0)
            nc.sync.dma_start(out=sim_view[b], in_=sim[:])

        def group_at(n, offset):
            i, t = divmod(n - offset, GROUP)
            return i if t == 0 and 0 <= i <= last else None

        def tile_at(n, offset):
            i, t = divmod(n - offset, GROUP)
            return (i, t) if 0 <= i <= last else None

        def exp_at(i):
            return 16 if i < last - 2 else 13

        def finish_at(i):
            return 19 if i < last - 2 else 16

        def on_gpsimd(i, t):
            return True

        def on_scalar(i, t):
            return i >= last - 2 and (False)

        def tiles_at(n, offset):
            pairs = []
            for i in range(len(items)):
                t = n - GROUP * i - (offset if isinstance(offset, int) else offset(i))
                if 0 <= t < GROUP:
                    pairs.append((i, t))
            return pairs

        for n in range(-12, GROUP * len(items) + 28):
            i = group_at(n, -12)
            if i is not None:
                load(i)
            for i, t in tiles_at(n, 8):
                if not is_keys(i):
                    multiply(i, t)
            for i, t in tiles_at(n, 3):
                if not is_keys(i) and t < 3:
                    gram(i, t)
            for i, t in tiles_at(n, 0):
                turn(i, t)
            for i, t in tiles_at(n, 2):
                regroup(i, t)
            for i, t in tiles_at(n, exp_at):
                if not is_keys(i):
                    exponential(i, t)
            for i, t in tiles_at(n, lambda i: finish_at(i) + 1):
                if not is_keys(i) and on_scalar(i, t):
                    normalise_on_scalar(i, t)
                    store(i, t, t + 1, nc.scalar)
            for i, t in tiles_at(n, 0):
                if not on_tensor(i, t):
                    square(i, t)
            for i, t in tiles_at(n, 10):
                if not is_keys(i):
                    scale(i, t)
            for i, t in tiles_at(n, 3):
                if is_keys(i):
                    if t == GROUP - 1:
                        quantise(i, 0, GROUP)
                elif (t + 1) % 4 == 0:
                    quantise(i, t + 1 - 4, t + 1)
            i = group_at(n, 6)
            if i is not None and not is_keys(i):
                diagonal(i)
            for i, t in tiles_at(n, lambda i: finish_at(i) - 2):
                if not is_keys(i):
                    if i < last - 2:
                        if (t + 1) % 2 == 0:
                            invert_row_sums(i, t + 1 - 2, t + 1)
            for i, t in tiles_at(n, 11):
                if not is_keys(i):
                    if i >= last - 2:
                        top(i, t, t + 1)
                        shift(i, t, t + 1, nc.gpsimd)
                    elif (t + 1) % 2 == 0:
                        top(i, t + 1 - 2, t + 1)
            for i, t in tiles_at(n, finish_at):
                if not is_keys(i):
                    if i >= last - 2:
                        invert_row_sums(i, t, t + 1)
                        if not on_scalar(i, t):
                            normalise(i, t, nc.vector)
                    elif not on_gpsimd(i, t):
                        normalise(i, t, nc.vector)
            i = group_at(n, 14)
            if i is not None and not is_keys(i) and i < last - 2:
                shift(i, 0, GROUP, nc.gpsimd)
            i = group_at(n, 6)
            if i is not None and not is_keys(i):
                norms(i)
            i = group_at(n, 4)
            if i is not None and is_keys(i):
                norms(i)
            i = group_at(n, 8)
            if i is not None and is_keys(i):
                spread_norms(i)
            i = group_at(n, 10)
            if i is not None and is_keys(i):
                keep_keys(i)
            for i, t in tiles_at(n, finish_at):
                if not is_keys(i):
                    if i < last - 2 and on_gpsimd(i, t):
                        normalise(i, t, nc.gpsimd)
                    if i < last - 2:
                        if t == GROUP - 1:
                            store(i, 0, GROUP)
                    elif not on_scalar(i, t):
                        store(i, t, t + 1)
            i = group_at(n, 18)
            if i is not None and not is_keys(i) and items[i]["g"] == GROUPS - 1:
                store_top(i)
